import numpy as np
import ml_dtypes

BF16 = ml_dtypes.bfloat16


def bf(x):
    return np.asarray(x, np.float32).astype(BF16)


def f32(x):
    return np.asarray(x, np.float32)


def f64(x):
    return np.asarray(x).astype(np.float64)


def striped(idx):
    return np.tile(idx.reshape(-1, 16).T, (8, 1))


C, D, P, S, N = 512, 256, 128, 512, 1024


def setup_inputs():
    return {"x": f32(0.6 * np.random.standard_normal((C, S))), "y": f32(0.6 * np.random.standard_normal((C, N))), "i_s": f32(0.6 * np.random.standard_normal((D, N))), "t_s": f32(0.6 * np.random.standard_normal((D, N))), "offs": striped(np.random.permutation(np.tile(np.arange(S), 2))[:N])}


def reference(x, y, i_s, t_s, offs):
    idx = offs[:16].T.reshape(-1)
    x, y = f64(x), f64(y)
    fx, tx = (x[:D] - x[D:])[:, idx], x[D:][:, idx]
    fy, ty = y[:D] - y[D:], y[D:]
    sg = f64(i_s) - f64(t_s)
    fr0, fi0, tr0, ti0 = fx[:P], fx[P:], tx[:P], tx[P:]
    fr1, fi1, tr1, ti1 = fy[:P], fy[P:], ty[:P], ty[P:]
    er = sg[:P] - (fr0 * tr1 + fi0 * ti1) - (tr0 * fr1 + ti0 * fi1)
    ei = sg[P:] - (fi0 * tr1 - fr0 * ti1) - (ti0 * fr1 - tr0 * fi1)
    return er * er + ei * ei

@@ -1,0 +1,84 @@
+import concourse.mybir as mybir
+
+P = 128
+S = 512
+N = 1024
+PIECE = 512
+F32 = mybir.dt.float32
+U16 = mybir.dt.uint16
+MULT = mybir.AluOpType.mult
+ADD = mybir.AluOpType.add
+SUB = mybir.AluOpType.subtract
+SQUARE = mybir.ActivationFunctionType.Square
+
+
+def tile_mseloss_kernel(tc, x, y, i_s, t_s, offs, out):
+    nc = tc.nc
+    with (
+        tc.tile_pool(name="held", bufs=1) as held,
+        tc.tile_pool(name="work", bufs=2) as work,
+    ):
+        offsets = held.tile([P, N // 16], U16, name="offsets")
+        nc.sync.dma_start(offsets[:], offs)
+
+        est_r0 = held.tile([P, S], F32, name="est_r0")
+        est_i0 = held.tile([P, S], F32, name="est_i0")
+        tr0 = held.tile([P, S], F32, name="tr0")
+        ti0 = held.tile([P, S], F32, name="ti0")
+        for block, tile in enumerate((est_r0, est_i0, tr0, ti0)):
+            nc.sync.dma_start(tile[:], x[block * P : (block + 1) * P, :])
+
+        fr0 = held.tile([P, S], F32, name="fr0")
+        fi0 = held.tile([P, S], F32, name="fi0")
+        nc.vector.tensor_tensor(fr0[:], est_r0[:], tr0[:], SUB)
+        nc.vector.tensor_tensor(fi0[:], est_i0[:], ti0[:], SUB)
+
+        for c in range(N // PIECE):
+            cols = slice(c * PIECE, (c + 1) * PIECE)
+            picks = offsets[:, c * PIECE // 16 : (c + 1) * PIECE // 16]
+
+            est_r1 = work.tile([P, PIECE], F32, name="est_r1")
+            est_i1 = work.tile([P, PIECE], F32, name="est_i1")
+            tr1 = work.tile([P, PIECE], F32, name="tr1")
+            ti1 = work.tile([P, PIECE], F32, name="ti1")
+            for block, tile in enumerate((est_r1, est_i1, tr1, ti1)):
+                nc.sync.dma_start(tile[:], y[block * P : (block + 1) * P, cols])
+            is_r = work.tile([P, PIECE], F32, name="is_r")
+            is_i = work.tile([P, PIECE], F32, name="is_i")
+            ts_r = work.tile([P, PIECE], F32, name="ts_r")
+            ts_i = work.tile([P, PIECE], F32, name="ts_i")
+            nc.scalar.dma_start(is_r[:], i_s[0:P, cols])
+            nc.scalar.dma_start(ts_r[:], t_s[0:P, cols])
+            nc.scalar.dma_start(is_i[:], i_s[P : 2 * P, cols])
+            nc.scalar.dma_start(ts_i[:], t_s[P : 2 * P, cols])
+
+            fr1 = work.tile([P, PIECE], F32, name="fr1")
+            fi1 = work.tile([P, PIECE], F32, name="fi1")
+            nc.vector.tensor_tensor(fr1[:], est_r1[:], tr1[:], SUB)
+            nc.vector.tensor_tensor(fi1[:], est_i1[:], ti1[:], SUB)
+
+            er = work.tile([P, PIECE], F32, name="er")
+            ei = work.tile([P, PIECE], F32, name="ei")
+            nc.vector.tensor_tensor(er[:], is_r[:], ts_r[:], SUB)
+            nc.vector.tensor_tensor(ei[:], is_i[:], ts_i[:], SUB)
+            for total, window, factor, sign in (
+                (er, fr0, tr1, SUB),
+                (er, fi0, ti1, SUB),
+                (er, tr0, fr1, SUB),
+                (er, ti0, fi1, SUB),
+                (ei, fi0, tr1, SUB),
+                (ei, fr0, ti1, ADD),
+                (ei, ti0, fr1, SUB),
+                (ei, tr0, fi1, ADD),
+            ):
+                product = work.tile([P, PIECE], F32, name="product")
+                nc.vector.tensor_tensor(product[:], window[:].indirect(picks), factor[:], MULT)
+                nc.vector.tensor_tensor(total[:], total[:], product[:], sign)
+
+            er_sq = work.tile([P, PIECE], F32, name="er_sq")
+            ei_sq = work.tile([P, PIECE], F32, name="ei_sq")
+            nc.scalar.activation(er_sq[:], er[:], SQUARE)
+            nc.scalar.activation(ei_sq[:], ei[:], SQUARE)
+            result = work.tile([P, PIECE], F32, name="result")
+            nc.vector.tensor_tensor(result[:], er_sq[:], ei_sq[:], ADD)
+            nc.sync.dma_start(out[:, cols], result[:])

@@ -1,9 +1,11 @@
 import concourse.mybir as mybir
+from concourse.masks import make_identity
 
 P = 128
 S = 512
 N = 1024
 PIECE = 512
+PIECES = N // PIECE
 F32 = mybir.dt.float32
 U16 = mybir.dt.uint16
 MULT = mybir.AluOpType.mult
@@ -16,69 +18,93 @@ def tile_mseloss_kernel(tc, x, y, i_s, t_s, offs, out):
     nc = tc.nc
     with (
         tc.tile_pool(name="held", bufs=1) as held,
-        tc.tile_pool(name="work", bufs=2) as work,
+        tc.tile_pool(name="ring", bufs=8) as ring,
+        tc.psum_pool(name="psum", bufs=1) as psum,
     ):
         offsets = held.tile([P, N // 16], U16, name="offsets")
         nc.sync.dma_start(offsets[:], offs)
 
-        est_r0 = held.tile([P, S], F32, name="est_r0")
-        est_i0 = held.tile([P, S], F32, name="est_i0")
-        tr0 = held.tile([P, S], F32, name="tr0")
-        ti0 = held.tile([P, S], F32, name="ti0")
-        for block, tile in enumerate((est_r0, est_i0, tr0, ti0)):
-            nc.sync.dma_start(tile[:], x[block * P : (block + 1) * P, :])
+        def store_tile(name):
+            return held.tile([P, S], F32, name=name)
 
-        fr0 = held.tile([P, S], F32, name="fr0")
-        fi0 = held.tile([P, S], F32, name="fi0")
+        def piece_tiles(name):
+            return [held.tile([P, PIECE], F32, name=f"{name}_{c}") for c in range(PIECES)]
+
+        def block(source, b, c):
+            return source[b * P : (b + 1) * P, c * PIECE : (c + 1) * PIECE]
+
+        est_r0, est_i0, tr0, ti0 = (store_tile(name) for name in ("est_r0", "est_i0", "tr0", "ti0"))
+        est_r1, est_i1, tr1, ti1 = (piece_tiles(name) for name in ("est_r1", "est_i1", "tr1", "ti1"))
+        is_r, is_i, ts_r, ts_i = (piece_tiles(name) for name in ("is_r", "is_i", "ts_r", "ts_i"))
+
+        loads = [
+            (tr0, x[2 * P : 3 * P, :]),
+            (est_r0, x[0:P, :]),
+            (tr1[0], block(y, 2, 0)),
+            (ti0, x[3 * P : 4 * P, :]),
+            (est_i0, x[P : 2 * P, :]),
+            (ti1[0], block(y, 3, 0)),
+        ]
+        for c in range(PIECES):
+            if c > 0:
+                loads += [(tr1[c], block(y, 2, c)), (ti1[c], block(y, 3, c))]
+            loads += [
+                (est_r1[c], block(y, 0, c)),
+                (est_i1[c], block(y, 1, c)),
+                (ts_r[c], block(t_s, 0, c)),
+                (is_r[c], block(i_s, 0, c)),
+                (ts_i[c], block(t_s, 1, c)),
+                (is_i[c], block(i_s, 1, c)),
+            ]
+        for k, (tile, rows) in enumerate(loads):
+            queue = nc.sync if k % 2 == 0 else nc.scalar
+            queue.dma_start(tile[:], rows)
+
+        plus = held.tile([P, P], F32, name="plus")
+        minus = held.tile([P, P], F32, name="minus")
+        make_identity(nc, plus[:])
+        nc.gpsimd.tensor_scalar_mul(minus[:], plus[:], -1.0)
+
+        fr0 = store_tile("fr0")
+        fi0 = store_tile("fi0")
         nc.vector.tensor_tensor(fr0[:], est_r0[:], tr0[:], SUB)
         nc.vector.tensor_tensor(fi0[:], est_i0[:], ti0[:], SUB)
 
-        for c in range(N // PIECE):
-            cols = slice(c * PIECE, (c + 1) * PIECE)
+        for c in range(PIECES):
             picks = offsets[:, c * PIECE // 16 : (c + 1) * PIECE // 16]
 
-            est_r1 = work.tile([P, PIECE], F32, name="est_r1")
-            est_i1 = work.tile([P, PIECE], F32, name="est_i1")
-            tr1 = work.tile([P, PIECE], F32, name="tr1")
-            ti1 = work.tile([P, PIECE], F32, name="ti1")
-            for block, tile in enumerate((est_r1, est_i1, tr1, ti1)):
-                nc.sync.dma_start(tile[:], y[block * P : (block + 1) * P, cols])
-            is_r = work.tile([P, PIECE], F32, name="is_r")
-            is_i = work.tile([P, PIECE], F32, name="is_i")
-            ts_r = work.tile([P, PIECE], F32, name="ts_r")
-            ts_i = work.tile([P, PIECE], F32, name="ts_i")
-            nc.scalar.dma_start(is_r[:], i_s[0:P, cols])
-            nc.scalar.dma_start(ts_r[:], t_s[0:P, cols])
-            nc.scalar.dma_start(is_i[:], i_s[P : 2 * P, cols])
-            nc.scalar.dma_start(ts_i[:], t_s[P : 2 * P, cols])
-
-            fr1 = work.tile([P, PIECE], F32, name="fr1")
-            fi1 = work.tile([P, PIECE], F32, name="fi1")
-            nc.vector.tensor_tensor(fr1[:], est_r1[:], tr1[:], SUB)
-            nc.vector.tensor_tensor(fi1[:], est_i1[:], ti1[:], SUB)
-
-            er = work.tile([P, PIECE], F32, name="er")
-            ei = work.tile([P, PIECE], F32, name="ei")
-            nc.vector.tensor_tensor(er[:], is_r[:], ts_r[:], SUB)
-            nc.vector.tensor_tensor(ei[:], is_i[:], ts_i[:], SUB)
-            for total, window, factor, sign in (
-                (er, fr0, tr1, SUB),
-                (er, fi0, ti1, SUB),
-                (er, tr0, fr1, SUB),
-                (er, ti0, fi1, SUB),
-                (ei, fi0, tr1, SUB),
-                (ei, fr0, ti1, ADD),
-                (ei, ti0, fr1, SUB),
-                (ei, tr0, fi1, ADD),
-            ):
-                product = work.tile([P, PIECE], F32, name="product")
+            def looked_up_product(window, factor):
+                product = ring.tile([P, PIECE], F32, name="product")
                 nc.vector.tensor_tensor(product[:], window[:].indirect(picks), factor[:], MULT)
-                nc.vector.tensor_tensor(total[:], total[:], product[:], sign)
+                return product
 
-            er_sq = work.tile([P, PIECE], F32, name="er_sq")
-            ei_sq = work.tile([P, PIECE], F32, name="ei_sq")
-            nc.scalar.activation(er_sq[:], er[:], SQUARE)
-            nc.scalar.activation(ei_sq[:], ei[:], SQUARE)
-            result = work.tile([P, PIECE], F32, name="result")
+            def on_gpsimd(name, left, right, op):
+                tile = held.tile([P, PIECE], F32, name=f"{name}_{c}")
+                nc.gpsimd.tensor_tensor(tile[:], left[:], right[:], op)
+                return tile
+
+            fr1 = on_gpsimd("fr1", est_r1[c], tr1[c], SUB)
+            fi1 = on_gpsimd("fi1", est_i1[c], ti1[c], SUB)
+            neg_sr = on_gpsimd("neg_sr", ts_r[c], is_r[c], SUB)
+            neg_si = on_gpsimd("neg_si", ts_i[c], is_i[c], SUB)
+
+            neg_er = psum.tile([P, PIECE], F32, name=f"neg_er_{c}")
+            neg_ei = psum.tile([P, PIECE], F32, name=f"neg_ei_{c}")
+            nc.tensor.matmul(neg_er[:], plus[:], looked_up_product(fr0, tr1[c])[:], start=True, stop=False)
+            nc.tensor.matmul(neg_ei[:], plus[:], looked_up_product(fi0, tr1[c])[:], start=True, stop=False)
+            nc.tensor.matmul(neg_er[:], plus[:], looked_up_product(fi0, ti1[c])[:], start=False, stop=False)
+            nc.tensor.matmul(neg_ei[:], minus[:], looked_up_product(fr0, ti1[c])[:], start=False, stop=False)
+            with_sr = on_gpsimd("with_sr", looked_up_product(tr0, fr1), neg_sr, ADD)
+            with_si = on_gpsimd("with_si", looked_up_product(ti0, fr1), neg_si, ADD)
+            nc.tensor.matmul(neg_er[:], plus[:], with_sr[:], start=False, stop=False)
+            nc.tensor.matmul(neg_ei[:], plus[:], with_si[:], start=False, stop=False)
+            nc.tensor.matmul(neg_er[:], plus[:], looked_up_product(ti0, fi1)[:], start=False, stop=True)
+            nc.tensor.matmul(neg_ei[:], minus[:], looked_up_product(tr0, fi1)[:], start=False, stop=True)
+
+            er_sq = held.tile([P, PIECE], F32, name=f"er_sq_{c}")
+            ei_sq = held.tile([P, PIECE], F32, name=f"ei_sq_{c}")
+            nc.scalar.activation(er_sq[:], neg_er[:], SQUARE)
+            nc.scalar.activation(ei_sq[:], neg_ei[:], SQUARE)
+            result = held.tile([P, PIECE], F32, name=f"result_{c}")
             nc.vector.tensor_tensor(result[:], er_sq[:], ei_sq[:], ADD)
-            nc.sync.dma_start(out[:, cols], result[:])
+            nc.sync.dma_start(out[:, c * PIECE : (c + 1) * PIECE], result[:])

@@ -78,15 +78,10 @@ def tile_mseloss_kernel(tc, x, y, i_s, t_s, offs, out):
                 nc.vector.tensor_tensor(product[:], window[:].indirect(picks), factor[:], MULT)
                 return product
 
-            def on_gpsimd(name, left, right, op):
+            def difference(name, left, right):
                 tile = held.tile([P, PIECE], F32, name=f"{name}_{c}")
-                nc.gpsimd.tensor_tensor(tile[:], left[:], right[:], op)
+                nc.vector.tensor_tensor(tile[:], left[:], right[:], SUB)
                 return tile
-
-            fr1 = on_gpsimd("fr1", est_r1[c], tr1[c], SUB)
-            fi1 = on_gpsimd("fi1", est_i1[c], ti1[c], SUB)
-            neg_sr = on_gpsimd("neg_sr", ts_r[c], is_r[c], SUB)
-            neg_si = on_gpsimd("neg_si", ts_i[c], is_i[c], SUB)
 
             neg_er = psum.tile([P, PIECE], F32, name=f"neg_er_{c}")
             neg_ei = psum.tile([P, PIECE], F32, name=f"neg_ei_{c}")
@@ -94,10 +89,12 @@ def tile_mseloss_kernel(tc, x, y, i_s, t_s, offs, out):
             nc.tensor.matmul(neg_ei[:], plus[:], looked_up_product(fi0, tr1[c])[:], start=True, stop=False)
             nc.tensor.matmul(neg_er[:], plus[:], looked_up_product(fi0, ti1[c])[:], start=False, stop=False)
             nc.tensor.matmul(neg_ei[:], minus[:], looked_up_product(fr0, ti1[c])[:], start=False, stop=False)
-            with_sr = on_gpsimd("with_sr", looked_up_product(tr0, fr1), neg_sr, ADD)
-            with_si = on_gpsimd("with_si", looked_up_product(ti0, fr1), neg_si, ADD)
-            nc.tensor.matmul(neg_er[:], plus[:], with_sr[:], start=False, stop=False)
-            nc.tensor.matmul(neg_ei[:], plus[:], with_si[:], start=False, stop=False)
+            fr1 = difference("fr1", est_r1[c], tr1[c])
+            fi1 = difference("fi1", est_i1[c], ti1[c])
+            nc.tensor.matmul(neg_er[:], plus[:], difference("neg_sr", ts_r[c], is_r[c])[:], start=False, stop=False)
+            nc.tensor.matmul(neg_ei[:], plus[:], difference("neg_si", ts_i[c], is_i[c])[:], start=False, stop=False)
+            nc.tensor.matmul(neg_er[:], plus[:], looked_up_product(tr0, fr1)[:], start=False, stop=False)
+            nc.tensor.matmul(neg_ei[:], plus[:], looked_up_product(ti0, fr1)[:], start=False, stop=False)
             nc.tensor.matmul(neg_er[:], plus[:], looked_up_product(ti0, fi1)[:], start=False, stop=True)
             nc.tensor.matmul(neg_ei[:], minus[:], looked_up_product(tr0, fi1)[:], start=False, stop=True)
 

@@ -4,8 +4,9 @@ from concourse.masks import make_identity
 P = 128
 S = 512
 N = 1024
-PIECE = 512
-PIECES = N // PIECE
+WIDTHS = (512, 384, 128)
+STARTS = tuple(sum(WIDTHS[:c]) for c in range(len(WIDTHS)))
+assert sum(WIDTHS) == N
 F32 = mybir.dt.float32
 U16 = mybir.dt.uint16
 MULT = mybir.AluOpType.mult
@@ -28,10 +29,10 @@ def tile_mseloss_kernel(tc, x, y, i_s, t_s, offs, out):
             return held.tile([P, S], F32, name=name)
 
         def piece_tiles(name):
-            return [held.tile([P, PIECE], F32, name=f"{name}_{c}") for c in range(PIECES)]
+            return [held.tile([P, width], F32, name=f"{name}_{c}") for c, width in enumerate(WIDTHS)]
 
         def block(source, b, c):
-            return source[b * P : (b + 1) * P, c * PIECE : (c + 1) * PIECE]
+            return source[b * P : (b + 1) * P, STARTS[c] : STARTS[c] + WIDTHS[c]]
 
         est_r0, est_i0, tr0, ti0 = (store_tile(name) for name in ("est_r0", "est_i0", "tr0", "ti0"))
         est_r1, est_i1, tr1, ti1 = (piece_tiles(name) for name in ("est_r1", "est_i1", "tr1", "ti1"))
@@ -41,11 +42,11 @@ def tile_mseloss_kernel(tc, x, y, i_s, t_s, offs, out):
             (tr0, x[2 * P : 3 * P, :]),
             (est_r0, x[0:P, :]),
             (tr1[0], block(y, 2, 0)),
+            (ti1[0], block(y, 3, 0)),
             (ti0, x[3 * P : 4 * P, :]),
             (est_i0, x[P : 2 * P, :]),
-            (ti1[0], block(y, 3, 0)),
         ]
-        for c in range(PIECES):
+        for c in range(len(WIDTHS)):
             if c > 0:
                 loads += [(tr1[c], block(y, 2, c)), (ti1[c], block(y, 3, c))]
             loads += [
@@ -70,38 +71,41 @@ def tile_mseloss_kernel(tc, x, y, i_s, t_s, offs, out):
         nc.vector.tensor_tensor(fr0[:], est_r0[:], tr0[:], SUB)
         nc.vector.tensor_tensor(fi0[:], est_i0[:], ti0[:], SUB)
 
-        for c in range(PIECES):
-            picks = offsets[:, c * PIECE // 16 : (c + 1) * PIECE // 16]
-
-            def looked_up_product(window, factor):
-                product = ring.tile([P, PIECE], F32, name="product")
-                nc.vector.tensor_tensor(product[:], window[:].indirect(picks), factor[:], MULT)
-                return product
+        for c, width in enumerate(WIDTHS):
+            picks = offsets[:, STARTS[c] // 16 : (STARTS[c] + width) // 16]
+            neg_er = psum.tile([P, width], F32, name=f"neg_er_{c}")
+            neg_ei = psum.tile([P, width], F32, name=f"neg_ei_{c}")
 
             def difference(name, left, right):
-                tile = held.tile([P, PIECE], F32, name=f"{name}_{c}")
+                tile = held.tile([P, width], F32, name=f"{name}_{c}")
                 nc.vector.tensor_tensor(tile[:], left[:], right[:], SUB)
                 return tile
 
-            neg_er = psum.tile([P, PIECE], F32, name=f"neg_er_{c}")
-            neg_ei = psum.tile([P, PIECE], F32, name=f"neg_ei_{c}")
-            nc.tensor.matmul(neg_er[:], plus[:], looked_up_product(fr0, tr1[c])[:], start=True, stop=False)
-            nc.tensor.matmul(neg_ei[:], plus[:], looked_up_product(fi0, tr1[c])[:], start=True, stop=False)
-            nc.tensor.matmul(neg_er[:], plus[:], looked_up_product(fi0, ti1[c])[:], start=False, stop=False)
-            nc.tensor.matmul(neg_ei[:], minus[:], looked_up_product(fr0, ti1[c])[:], start=False, stop=False)
+            def looked_up_product(window, factor):
+                product = ring.tile([P, width], F32, name="product")
+                nc.vector.tensor_tensor(product[:], window[:].indirect(picks), factor[:], MULT)
+                return product
+
+            def collect(total, weights, term, start=False, stop=False):
+                nc.tensor.matmul(total[:], weights[:], term[:], start=start, stop=stop)
+
+            collect(neg_er, plus, looked_up_product(fr0, tr1[c]), start=True)
+            collect(neg_ei, minus, looked_up_product(fr0, ti1[c]), start=True)
+            collect(neg_ei, plus, looked_up_product(fi0, tr1[c]))
+            collect(neg_er, plus, looked_up_product(fi0, ti1[c]))
+            collect(neg_er, plus, difference("neg_sr", ts_r[c], is_r[c]))
+            collect(neg_ei, plus, difference("neg_si", ts_i[c], is_i[c]))
             fr1 = difference("fr1", est_r1[c], tr1[c])
             fi1 = difference("fi1", est_i1[c], ti1[c])
-            nc.tensor.matmul(neg_er[:], plus[:], difference("neg_sr", ts_r[c], is_r[c])[:], start=False, stop=False)
-            nc.tensor.matmul(neg_ei[:], plus[:], difference("neg_si", ts_i[c], is_i[c])[:], start=False, stop=False)
-            nc.tensor.matmul(neg_er[:], plus[:], looked_up_product(tr0, fr1)[:], start=False, stop=False)
-            nc.tensor.matmul(neg_ei[:], plus[:], looked_up_product(ti0, fr1)[:], start=False, stop=False)
-            nc.tensor.matmul(neg_er[:], plus[:], looked_up_product(ti0, fi1)[:], start=False, stop=True)
-            nc.tensor.matmul(neg_ei[:], minus[:], looked_up_product(tr0, fi1)[:], start=False, stop=True)
+            collect(neg_er, plus, looked_up_product(tr0, fr1))
+            collect(neg_ei, plus, looked_up_product(ti0, fr1))
+            collect(neg_er, plus, looked_up_product(ti0, fi1), stop=True)
+            collect(neg_ei, minus, looked_up_product(tr0, fi1), stop=True)
 
-            er_sq = held.tile([P, PIECE], F32, name=f"er_sq_{c}")
-            ei_sq = held.tile([P, PIECE], F32, name=f"ei_sq_{c}")
+            er_sq = held.tile([P, width], F32, name=f"er_sq_{c}")
+            ei_sq = held.tile([P, width], F32, name=f"ei_sq_{c}")
             nc.scalar.activation(er_sq[:], neg_er[:], SQUARE)
             nc.scalar.activation(ei_sq[:], neg_ei[:], SQUARE)
-            result = held.tile([P, PIECE], F32, name=f"result_{c}")
+            result = held.tile([P, width], F32, name=f"result_{c}")
             nc.vector.tensor_tensor(result[:], er_sq[:], ei_sq[:], ADD)
-            nc.sync.dma_start(out[:, c * PIECE : (c + 1) * PIECE], result[:])
+            nc.sync.dma_start(out[:, STARTS[c] : STARTS[c] + width], result[:])

@@ -4,15 +4,18 @@ from concourse.masks import make_identity
 P = 128
 S = 512
 N = 1024
+BLOCK = 128
+BANK = 512
 WIDTHS = (512, 384, 128)
 STARTS = tuple(sum(WIDTHS[:c]) for c in range(len(WIDTHS)))
 assert sum(WIDTHS) == N
 F32 = mybir.dt.float32
 U16 = mybir.dt.uint16
 MULT = mybir.AluOpType.mult
-ADD = mybir.AluOpType.add
 SUB = mybir.AluOpType.subtract
 SQUARE = mybir.ActivationFunctionType.Square
+COPY = mybir.ActivationFunctionType.Copy
+REAL, IMAG = 0, 1
 
 
 def tile_mseloss_kernel(tc, x, y, i_s, t_s, offs, out):
@@ -20,92 +23,127 @@ def tile_mseloss_kernel(tc, x, y, i_s, t_s, offs, out):
     with (
         tc.tile_pool(name="held", bufs=1) as held,
         tc.tile_pool(name="ring", bufs=8) as ring,
-        tc.psum_pool(name="psum", bufs=1) as psum,
+        tc.psum_pool(name="psum", bufs=2) as psum,
     ):
         offsets = held.tile([P, N // 16], U16, name="offsets")
-        nc.sync.dma_start(offsets[:], offs)
 
         def store_tile(name):
             return held.tile([P, S], F32, name=name)
 
-        def piece_tiles(name):
-            return [held.tile([P, width], F32, name=f"{name}_{c}") for c, width in enumerate(WIDTHS)]
+        def pair_tiles(name):
+            return [held.tile([P, 2, width], F32, name=f"{name}_{c}") for c, width in enumerate(WIDTHS)]
 
-        def block(source, b, c):
-            return source[b * P : (b + 1) * P, STARTS[c] : STARTS[c] + WIDTHS[c]]
+        def rows(source, first_block, c):
+            columns = source[first_block * P : (first_block + 2) * P, STARTS[c] : STARTS[c] + WIDTHS[c]]
+            return columns.rearrange("(b p) w -> p b w", p=P)
 
         est_r0, est_i0, tr0, ti0 = (store_tile(name) for name in ("est_r0", "est_i0", "tr0", "ti0"))
-        est_r1, est_i1, tr1, ti1 = (piece_tiles(name) for name in ("est_r1", "est_i1", "tr1", "ti1"))
-        is_r, is_i, ts_r, ts_i = (piece_tiles(name) for name in ("is_r", "is_i", "ts_r", "ts_i"))
+        est1, t1, i_s1, t_s1 = (pair_tiles(name) for name in ("est1", "t1", "i_s1", "t_s1"))
 
-        loads = [
-            (tr0, x[2 * P : 3 * P, :]),
-            (est_r0, x[0:P, :]),
-            (tr1[0], block(y, 2, 0)),
-            (ti1[0], block(y, 3, 0)),
-            (ti0, x[3 * P : 4 * P, :]),
-            (est_i0, x[P : 2 * P, :]),
-        ]
+        nc.sync.dma_start(tr0[:], x[2 * P : 3 * P, :])
+        nc.scalar.dma_start(est_r0[:], x[0:P, :])
+        nc.sync.dma_start(offsets[:], offs)
+        nc.scalar.dma_start(t1[0][:, REAL, :], y[2 * P : 3 * P, 0 : WIDTHS[0]])
+        nc.sync.dma_start(t1[0][:, IMAG, :], y[3 * P : 4 * P, 0 : WIDTHS[0]])
+        nc.scalar.dma_start(ti0[:], x[3 * P : 4 * P, :])
+        nc.sync.dma_start(est_i0[:], x[P : 2 * P, :])
         for c in range(len(WIDTHS)):
             if c > 0:
-                loads += [(tr1[c], block(y, 2, c)), (ti1[c], block(y, 3, c))]
-            loads += [
-                (est_r1[c], block(y, 0, c)),
-                (est_i1[c], block(y, 1, c)),
-                (ts_r[c], block(t_s, 0, c)),
-                (is_r[c], block(i_s, 0, c)),
-                (ts_i[c], block(t_s, 1, c)),
-                (is_i[c], block(i_s, 1, c)),
-            ]
-        for k, (tile, rows) in enumerate(loads):
-            queue = nc.sync if k % 2 == 0 else nc.scalar
-            queue.dma_start(tile[:], rows)
+                nc.sync.dma_start(t1[c][:], rows(y, 2, c))
+            nc.sync.dma_start(est1[c][:], rows(y, 0, c))
+            nc.sync.dma_start(t_s1[c][:], rows(t_s, 0, c))
+            nc.sync.dma_start(i_s1[c][:], rows(i_s, 0, c))
 
-        plus = held.tile([P, P], F32, name="plus")
-        minus = held.tile([P, P], F32, name="minus")
-        make_identity(nc, plus[:])
-        nc.gpsimd.tensor_scalar_mul(minus[:], plus[:], -1.0)
+        identity = held.tile([P, P], F32, name="identity")
+        make_identity(nc, identity[:])
 
         fr0 = store_tile("fr0")
         fi0 = store_tile("fi0")
         nc.vector.tensor_tensor(fr0[:], est_r0[:], tr0[:], SUB)
         nc.vector.tensor_tensor(fi0[:], est_i0[:], ti0[:], SUB)
 
-        for c, width in enumerate(WIDTHS):
-            picks = offsets[:, STARTS[c] // 16 : (STARTS[c] + width) // 16]
-            neg_er = psum.tile([P, width], F32, name=f"neg_er_{c}")
-            neg_ei = psum.tile([P, width], F32, name=f"neg_ei_{c}")
+        def blocks(c):
+            return [slice(b * BLOCK, (b + 1) * BLOCK) for b in range(WIDTHS[c] // BLOCK)]
 
-            def difference(name, left, right):
-                tile = held.tile([P, width], F32, name=f"{name}_{c}")
-                nc.vector.tensor_tensor(tile[:], left[:], right[:], SUB)
-                return tile
+        def add_transposed(c, bank, term, first=False, last=False):
+            for b in blocks(c):
+                nc.tensor.matmul(
+                    bank[:, b],
+                    lhsT=term[:, b],
+                    rhs=identity[:],
+                    is_transpose=True,
+                    start=first and b == blocks(c)[0],
+                    stop=last and b == blocks(c)[-1],
+                )
 
-            def looked_up_product(window, factor):
-                product = ring.tile([P, width], F32, name="product")
-                nc.vector.tensor_tensor(product[:], window[:].indirect(picks), factor[:], MULT)
-                return product
+        def looked_up_product(c, window, factor):
+            picks = offsets[:, STARTS[c] // 16 : (STARTS[c] + WIDTHS[c]) // 16]
+            product = ring.tile([P, WIDTHS[c]], F32, name="product")
+            nc.vector.tensor_tensor(product[:], window[:].indirect(picks), factor, MULT)
+            return product
 
-            def collect(total, weights, term, start=False, stop=False):
-                nc.tensor.matmul(total[:], weights[:], term[:], start=start, stop=stop)
+        def negated(name, source, shape):
+            tile = held.tile(shape, F32, name=name)
+            nc.scalar.activation(tile[:], source, COPY, scale=-1.0)
+            return tile
 
-            collect(neg_er, plus, looked_up_product(fr0, tr1[c]), start=True)
-            collect(neg_ei, minus, looked_up_product(fr0, ti1[c]), start=True)
-            collect(neg_ei, plus, looked_up_product(fi0, tr1[c]))
-            collect(neg_er, plus, looked_up_product(fi0, ti1[c]))
-            collect(neg_er, plus, difference("neg_sr", ts_r[c], is_r[c]))
-            collect(neg_ei, plus, difference("neg_si", ts_i[c], is_i[c]))
-            fr1 = difference("fr1", est_r1[c], tr1[c])
-            fi1 = difference("fi1", est_i1[c], ti1[c])
-            collect(neg_er, plus, looked_up_product(tr0, fr1))
-            collect(neg_ei, plus, looked_up_product(ti0, fr1))
-            collect(neg_er, plus, looked_up_product(ti0, fi1), stop=True)
-            collect(neg_ei, minus, looked_up_product(tr0, fi1), stop=True)
+        factors = {}
+        sums = {}
 
+        def prepare(c):
+            width = WIDTHS[c]
+            neg_ti1 = negated(f"neg_ti1_{c}", t1[c][:, IMAG, :], [P, width])
+            f1 = held.tile([P, 2, width], F32, name=f"f1_{c}")
+            nc.vector.tensor_tensor(f1[:], est1[c][:], t1[c][:], SUB)
+            neg_fi1 = negated(f"neg_fi1_{c}", f1[:, IMAG, :], [P, width])
+            neg_i_s = negated(f"neg_i_s_{c}", i_s1[c][:], [P, 2, width])
+            factors[c] = (neg_ti1, f1, neg_fi1, neg_i_s)
+
+        def first_half(c):
+            neg_ti1, f1, neg_fi1, neg_i_s = factors[c]
+            tr1, ti1 = t1[c][:, REAL, :], t1[c][:, IMAG, :]
+            neg_er = psum.tile([P, BANK], F32, name="neg_er")
+            neg_ei = psum.tile([P, BANK], F32, name="neg_ei")
+            sums[c] = (neg_er, neg_ei)
+            add_transposed(c, neg_er, looked_up_product(c, fr0, tr1), first=True)
+            add_transposed(c, neg_ei, looked_up_product(c, fr0, neg_ti1[:]), first=True)
+            add_transposed(c, neg_ei, looked_up_product(c, fi0, tr1))
+            add_transposed(c, neg_er, looked_up_product(c, fi0, ti1))
+            add_transposed(c, neg_er, t_s1[c][:, REAL, :])
+            add_transposed(c, neg_er, neg_i_s[:, REAL, :])
+            add_transposed(c, neg_ei, t_s1[c][:, IMAG, :])
+            add_transposed(c, neg_ei, neg_i_s[:, IMAG, :])
+
+        def second_half(c):
+            neg_ti1, f1, neg_fi1, neg_i_s = factors[c]
+            neg_er, neg_ei = sums[c]
+            fr1, fi1 = f1[:, REAL, :], f1[:, IMAG, :]
+            add_transposed(c, neg_er, looked_up_product(c, tr0, fr1))
+            add_transposed(c, neg_ei, looked_up_product(c, ti0, fr1))
+            add_transposed(c, neg_er, looked_up_product(c, ti0, fi1), last=True)
+            add_transposed(c, neg_ei, looked_up_product(c, tr0, neg_fi1[:]), last=True)
+
+        def finish(c):
+            width = WIDTHS[c]
+            neg_er, neg_ei = sums[c]
             er_sq = held.tile([P, width], F32, name=f"er_sq_{c}")
             ei_sq = held.tile([P, width], F32, name=f"ei_sq_{c}")
-            nc.scalar.activation(er_sq[:], neg_er[:], SQUARE)
-            nc.scalar.activation(ei_sq[:], neg_ei[:], SQUARE)
+            nc.scalar.activation(er_sq[:], neg_er[:, 0:width], SQUARE)
+            nc.scalar.activation(ei_sq[:], neg_ei[:, 0:width], SQUARE)
+            total = psum.tile([P, BANK], F32, name="total")
+            add_transposed(c, total, er_sq, first=True)
+            add_transposed(c, total, ei_sq, last=True)
             result = held.tile([P, width], F32, name=f"result_{c}")
-            nc.vector.tensor_tensor(result[:], er_sq[:], ei_sq[:], ADD)
+            nc.scalar.activation(result[:], total[:, 0:width], COPY)
             nc.sync.dma_start(out[:, STARTS[c] : STARTS[c] + width], result[:])
+
+        pieces = range(len(WIDTHS))
+        prepare(0)
+        for c in pieces:
+            first_half(c)
+            if c > 0:
+                finish(c - 1)
+            if c + 1 < len(WIDTHS):
+                prepare(c + 1)
+            second_half(c)
+        finish(len(WIDTHS) - 1)

@@ -55,7 +55,9 @@ def tile_mseloss_kernel(tc, x, y, i_s, t_s, offs, out):
             nc.sync.dma_start(i_s1[c][:], rows(i_s, 0, c))
 
         identity = held.tile([P, P], F32, name="identity")
+        minus = held.tile([P, P], F32, name="minus")
         make_identity(nc, identity[:])
+        nc.gpsimd.tensor_scalar_mul(minus[:], identity[:], -1.0)
 
         fr0 = store_tile("fr0")
         fi0 = store_tile("fi0")
@@ -94,8 +96,16 @@ def tile_mseloss_kernel(tc, x, y, i_s, t_s, offs, out):
             width = WIDTHS[c]
             neg_ti1 = negated(f"neg_ti1_{c}", t1[c][:, IMAG, :], [P, width])
             f1 = held.tile([P, 2, width], F32, name=f"f1_{c}")
-            nc.vector.tensor_tensor(f1[:], est1[c][:], t1[c][:], SUB)
-            neg_fi1 = negated(f"neg_fi1_{c}", f1[:, IMAG, :], [P, width])
+            if c == 0:
+                nc.vector.tensor_tensor(f1[:], est1[c][:], t1[c][:], SUB)
+                neg_fi1 = negated(f"neg_fi1_{c}", f1[:, IMAG, :], [P, width])
+            else:
+                for part in (REAL, IMAG):
+                    gap = psum.tile([P, BANK], F32, name="gap")
+                    nc.tensor.matmul(gap[:, 0:width], identity[:], est1[c][:, part, :], start=True, stop=False)
+                    nc.tensor.matmul(gap[:, 0:width], minus[:], t1[c][:, part, :], start=False, stop=True)
+                    nc.scalar.activation(f1[:, part, :], gap[:, 0:width], COPY)
+                neg_fi1 = negated(f"neg_fi1_{c}", gap[:, 0:width], [P, width])
             neg_i_s = negated(f"neg_i_s_{c}", i_s1[c][:], [P, 2, width])
             factors[c] = (neg_ti1, f1, neg_fi1, neg_i_s)
 

@@ -94,52 +94,54 @@ def tile_mseloss_kernel(tc, x, y, i_s, t_s, offs, out):
 
         def prepare(c):
             width = WIDTHS[c]
-            neg_ti1 = negated(f"neg_ti1_{c}", t1[c][:, IMAG, :], [P, width])
+            neg_tr1 = negated(f"neg_tr1_{c}", t1[c][:, REAL, :], [P, width])
             f1 = held.tile([P, 2, width], F32, name=f"f1_{c}")
             if c == 0:
                 nc.vector.tensor_tensor(f1[:], est1[c][:], t1[c][:], SUB)
-                neg_fi1 = negated(f"neg_fi1_{c}", f1[:, IMAG, :], [P, width])
+                neg_fr1 = negated(f"neg_fr1_{c}", f1[:, REAL, :], [P, width])
             else:
                 for part in (REAL, IMAG):
                     gap = psum.tile([P, BANK], F32, name="gap")
                     nc.tensor.matmul(gap[:, 0:width], identity[:], est1[c][:, part, :], start=True, stop=False)
                     nc.tensor.matmul(gap[:, 0:width], minus[:], t1[c][:, part, :], start=False, stop=True)
                     nc.scalar.activation(f1[:, part, :], gap[:, 0:width], COPY)
-                neg_fi1 = negated(f"neg_fi1_{c}", gap[:, 0:width], [P, width])
-            neg_i_s = negated(f"neg_i_s_{c}", i_s1[c][:], [P, 2, width])
-            factors[c] = (neg_ti1, f1, neg_fi1, neg_i_s)
+                    if part == REAL:
+                        neg_fr1 = negated(f"neg_fr1_{c}", gap[:, 0:width], [P, width])
+            neg_is_r = negated(f"neg_is_r_{c}", i_s1[c][:, REAL, :], [P, width])
+            neg_ts_i = negated(f"neg_ts_i_{c}", t_s1[c][:, IMAG, :], [P, width])
+            factors[c] = (neg_tr1, f1, neg_fr1, neg_is_r, neg_ts_i)
 
         def first_half(c):
-            neg_ti1, f1, neg_fi1, neg_i_s = factors[c]
+            neg_tr1, f1, neg_fr1, neg_is_r, neg_ts_i = factors[c]
             tr1, ti1 = t1[c][:, REAL, :], t1[c][:, IMAG, :]
             neg_er = psum.tile([P, BANK], F32, name="neg_er")
-            neg_ei = psum.tile([P, BANK], F32, name="neg_ei")
-            sums[c] = (neg_er, neg_ei)
+            pos_ei = psum.tile([P, BANK], F32, name="pos_ei")
+            sums[c] = (neg_er, pos_ei)
             add_transposed(c, neg_er, looked_up_product(c, fr0, tr1), first=True)
-            add_transposed(c, neg_ei, looked_up_product(c, fr0, neg_ti1[:]), first=True)
-            add_transposed(c, neg_ei, looked_up_product(c, fi0, tr1))
+            add_transposed(c, pos_ei, looked_up_product(c, fr0, ti1), first=True)
+            add_transposed(c, pos_ei, looked_up_product(c, fi0, neg_tr1[:]))
             add_transposed(c, neg_er, looked_up_product(c, fi0, ti1))
             add_transposed(c, neg_er, t_s1[c][:, REAL, :])
-            add_transposed(c, neg_er, neg_i_s[:, REAL, :])
-            add_transposed(c, neg_ei, t_s1[c][:, IMAG, :])
-            add_transposed(c, neg_ei, neg_i_s[:, IMAG, :])
+            add_transposed(c, neg_er, neg_is_r[:])
+            add_transposed(c, pos_ei, i_s1[c][:, IMAG, :])
+            add_transposed(c, pos_ei, neg_ts_i[:])
 
         def second_half(c):
-            neg_ti1, f1, neg_fi1, neg_i_s = factors[c]
-            neg_er, neg_ei = sums[c]
+            neg_tr1, f1, neg_fr1, neg_is_r, neg_ts_i = factors[c]
+            neg_er, pos_ei = sums[c]
             fr1, fi1 = f1[:, REAL, :], f1[:, IMAG, :]
             add_transposed(c, neg_er, looked_up_product(c, tr0, fr1))
-            add_transposed(c, neg_ei, looked_up_product(c, ti0, fr1))
+            add_transposed(c, pos_ei, looked_up_product(c, tr0, fi1))
             add_transposed(c, neg_er, looked_up_product(c, ti0, fi1), last=True)
-            add_transposed(c, neg_ei, looked_up_product(c, tr0, neg_fi1[:]), last=True)
+            add_transposed(c, pos_ei, looked_up_product(c, ti0, neg_fr1[:]), last=True)
 
         def finish(c):
             width = WIDTHS[c]
-            neg_er, neg_ei = sums[c]
+            neg_er, pos_ei = sums[c]
             er_sq = held.tile([P, width], F32, name=f"er_sq_{c}")
             ei_sq = held.tile([P, width], F32, name=f"ei_sq_{c}")
             nc.scalar.activation(er_sq[:], neg_er[:, 0:width], SQUARE)
-            nc.scalar.activation(ei_sq[:], neg_ei[:, 0:width], SQUARE)
+            nc.scalar.activation(ei_sq[:], pos_ei[:, 0:width], SQUARE)
             total = psum.tile([P, BANK], F32, name="total")
             add_transposed(c, total, er_sq, first=True)
             add_transposed(c, total, ei_sq, last=True)

@@ -62,7 +62,6 @@ def tile_mseloss_kernel(tc, x, y, i_s, t_s, offs, out):
         fr0 = store_tile("fr0")
         fi0 = store_tile("fi0")
         nc.vector.tensor_tensor(fr0[:], est_r0[:], tr0[:], SUB)
-        nc.vector.tensor_tensor(fi0[:], est_i0[:], ti0[:], SUB)
 
         def blocks(c):
             return [slice(b * BLOCK, (b + 1) * BLOCK) for b in range(WIDTHS[c] // BLOCK)]
@@ -89,6 +88,17 @@ def tile_mseloss_kernel(tc, x, y, i_s, t_s, offs, out):
             nc.scalar.activation(tile[:], source, COPY, scale=-1.0)
             return tile
 
+        assert S == WIDTHS[0]
+        neg_ti0 = negated("neg_ti0", ti0[:], [P, S])
+        fi0_turned_sum = psum.tile([P, BANK], F32, name="gap")
+        add_transposed(0, fi0_turned_sum, est_i0, first=True)
+        add_transposed(0, fi0_turned_sum, neg_ti0, last=True)
+        fi0_turned = store_tile("fi0_turned")
+        nc.scalar.activation(fi0_turned[:], fi0_turned_sum[:], COPY)
+        fi0_back = psum.tile([P, BANK], F32, name="gap")
+        add_transposed(0, fi0_back, fi0_turned, first=True, last=True)
+        nc.scalar.activation(fi0[:], fi0_back[:], COPY)
+
         factors = {}
         sums = {}
 
@@ -111,29 +121,36 @@ def tile_mseloss_kernel(tc, x, y, i_s, t_s, offs, out):
             neg_ts_i = negated(f"neg_ts_i_{c}", t_s1[c][:, IMAG, :], [P, width])
             factors[c] = (neg_tr1, f1, neg_fr1, neg_is_r, neg_ts_i)
 
-        def first_half(c):
-            neg_tr1, f1, neg_fr1, neg_is_r, neg_ts_i = factors[c]
+        def real_gap_products(c):
             tr1, ti1 = t1[c][:, REAL, :], t1[c][:, IMAG, :]
             neg_er = psum.tile([P, BANK], F32, name="neg_er")
             pos_ei = psum.tile([P, BANK], F32, name="pos_ei")
             sums[c] = (neg_er, pos_ei)
             add_transposed(c, neg_er, looked_up_product(c, fr0, tr1), first=True)
             add_transposed(c, pos_ei, looked_up_product(c, fr0, ti1), first=True)
-            add_transposed(c, pos_ei, looked_up_product(c, fi0, neg_tr1[:]))
-            add_transposed(c, neg_er, looked_up_product(c, fi0, ti1))
+
+        def imaginary_gap_products(c, last):
+            neg_tr1, f1, neg_fr1, neg_is_r, neg_ts_i = factors[c]
+            neg_er, pos_ei = sums[c]
+            add_transposed(c, pos_ei, looked_up_product(c, fi0, neg_tr1[:]), last=last)
+            add_transposed(c, neg_er, looked_up_product(c, fi0, t1[c][:, IMAG, :]), last=last)
+
+        def second_order(c):
+            neg_tr1, f1, neg_fr1, neg_is_r, neg_ts_i = factors[c]
+            neg_er, pos_ei = sums[c]
             add_transposed(c, neg_er, t_s1[c][:, REAL, :])
             add_transposed(c, neg_er, neg_is_r[:])
             add_transposed(c, pos_ei, i_s1[c][:, IMAG, :])
             add_transposed(c, pos_ei, neg_ts_i[:])
 
-        def second_half(c):
+        def target_products(c, last):
             neg_tr1, f1, neg_fr1, neg_is_r, neg_ts_i = factors[c]
             neg_er, pos_ei = sums[c]
             fr1, fi1 = f1[:, REAL, :], f1[:, IMAG, :]
             add_transposed(c, neg_er, looked_up_product(c, tr0, fr1))
             add_transposed(c, pos_ei, looked_up_product(c, tr0, fi1))
-            add_transposed(c, neg_er, looked_up_product(c, ti0, fi1), last=True)
-            add_transposed(c, pos_ei, looked_up_product(c, ti0, neg_fr1[:]), last=True)
+            add_transposed(c, neg_er, looked_up_product(c, ti0, fi1), last=last)
+            add_transposed(c, pos_ei, looked_up_product(c, ti0, neg_fr1[:]), last=last)
 
         def finish(c):
             width = WIDTHS[c]
@@ -149,13 +166,18 @@ def tile_mseloss_kernel(tc, x, y, i_s, t_s, offs, out):
             nc.scalar.activation(result[:], total[:, 0:width], COPY)
             nc.sync.dma_start(out[:, STARTS[c] : STARTS[c] + width], result[:])
 
-        pieces = range(len(WIDTHS))
         prepare(0)
-        for c in pieces:
-            first_half(c)
-            if c > 0:
-                finish(c - 1)
+        real_gap_products(0)
+        target_products(0, last=False)
+        second_order(0)
+        prepare(1)
+        imaginary_gap_products(0, last=True)
+        for c in range(1, len(WIDTHS)):
+            real_gap_products(c)
+            imaginary_gap_products(c, last=False)
+            second_order(c)
+            finish(c - 1)
             if c + 1 < len(WIDTHS):
                 prepare(c + 1)
-            second_half(c)
+            target_products(c, last=True)
         finish(len(WIDTHS) - 1)

@@ -47,10 +47,11 @@ def tile_mseloss_kernel(tc, x, y, i_s, t_s, offs, out):
         nc.sync.dma_start(t1[0][:, IMAG, :], y[3 * P : 4 * P, 0 : WIDTHS[0]])
         nc.scalar.dma_start(ti0[:], x[3 * P : 4 * P, :])
         nc.sync.dma_start(est_i0[:], x[P : 2 * P, :])
+        nc.sync.dma_start(est1[0][:], rows(y, 0, 0))
         for c in range(len(WIDTHS)):
-            if c > 0:
-                nc.sync.dma_start(t1[c][:], rows(y, 2, c))
-            nc.sync.dma_start(est1[c][:], rows(y, 0, c))
+            if c + 1 < len(WIDTHS):
+                nc.sync.dma_start(t1[c + 1][:], rows(y, 2, c + 1))
+                nc.sync.dma_start(est1[c + 1][:], rows(y, 0, c + 1))
             nc.sync.dma_start(t_s1[c][:], rows(t_s, 0, c))
             nc.sync.dma_start(i_s1[c][:], rows(i_s, 0, c))
 
@@ -110,16 +111,24 @@ def tile_mseloss_kernel(tc, x, y, i_s, t_s, offs, out):
                 nc.vector.tensor_tensor(f1[:], est1[c][:], t1[c][:], SUB)
                 neg_fr1 = negated(f"neg_fr1_{c}", f1[:, REAL, :], [P, width])
             else:
-                for part in (REAL, IMAG):
-                    gap = psum.tile([P, BANK], F32, name="gap")
-                    nc.tensor.matmul(gap[:, 0:width], identity[:], est1[c][:, part, :], start=True, stop=False)
-                    nc.tensor.matmul(gap[:, 0:width], minus[:], t1[c][:, part, :], start=False, stop=True)
-                    nc.scalar.activation(f1[:, part, :], gap[:, 0:width], COPY)
-                    if part == REAL:
-                        neg_fr1 = negated(f"neg_fr1_{c}", gap[:, 0:width], [P, width])
-            neg_is_r = negated(f"neg_is_r_{c}", i_s1[c][:, REAL, :], [P, width])
-            neg_ts_i = negated(f"neg_ts_i_{c}", t_s1[c][:, IMAG, :], [P, width])
-            factors[c] = (neg_tr1, f1, neg_fr1, neg_is_r, neg_ts_i)
+                neg_fr1 = held.tile([P, width], F32, name=f"neg_fr1_{c}")
+            factors[c] = (neg_tr1, f1, neg_fr1)
+
+        gap_blocks = [(c, part, b) for c in range(1, len(WIDTHS)) for part in (REAL, IMAG) for b in blocks(c)]
+        blocks_made = []
+
+        def next_gap_block():
+            if len(blocks_made) == len(gap_blocks):
+                return
+            c, part, b = gap_blocks[len(blocks_made)]
+            blocks_made.append((c, part, b))
+            neg_tr1, f1, neg_fr1 = factors[c]
+            gap = psum.tile([P, BANK], F32, name="gap")
+            nc.tensor.matmul(gap[:, 0:BLOCK], identity[:], est1[c][:, part, b], start=True, stop=False)
+            nc.tensor.matmul(gap[:, 0:BLOCK], minus[:], t1[c][:, part, b], start=False, stop=True)
+            nc.scalar.activation(f1[:, part, b], gap[:, 0:BLOCK], COPY)
+            if part == REAL:
+                nc.scalar.activation(neg_fr1[:, b], gap[:, 0:BLOCK], COPY, scale=-1.0)
 
         def real_gap_products(c):
             tr1, ti1 = t1[c][:, REAL, :], t1[c][:, IMAG, :]
@@ -129,28 +138,38 @@ def tile_mseloss_kernel(tc, x, y, i_s, t_s, offs, out):
             add_transposed(c, neg_er, looked_up_product(c, fr0, tr1), first=True)
             add_transposed(c, pos_ei, looked_up_product(c, fr0, ti1), first=True)
 
-        def imaginary_gap_products(c, last):
-            neg_tr1, f1, neg_fr1, neg_is_r, neg_ts_i = factors[c]
+        def nothing():
+            return None
+
+        def imaginary_gap_products(c, last, after_each):
+            neg_tr1, f1, neg_fr1 = factors[c]
             neg_er, pos_ei = sums[c]
             add_transposed(c, pos_ei, looked_up_product(c, fi0, neg_tr1[:]), last=last)
+            after_each()
             add_transposed(c, neg_er, looked_up_product(c, fi0, t1[c][:, IMAG, :]), last=last)
+            after_each()
 
         def second_order(c):
-            neg_tr1, f1, neg_fr1, neg_is_r, neg_ts_i = factors[c]
             neg_er, pos_ei = sums[c]
+            neg_is_r = negated(f"neg_is_r_{c}", i_s1[c][:, REAL, :], [P, WIDTHS[c]])
+            neg_ts_i = negated(f"neg_ts_i_{c}", t_s1[c][:, IMAG, :], [P, WIDTHS[c]])
             add_transposed(c, neg_er, t_s1[c][:, REAL, :])
             add_transposed(c, neg_er, neg_is_r[:])
             add_transposed(c, pos_ei, i_s1[c][:, IMAG, :])
             add_transposed(c, pos_ei, neg_ts_i[:])
 
-        def target_products(c, last):
-            neg_tr1, f1, neg_fr1, neg_is_r, neg_ts_i = factors[c]
+        def target_products(c, last, after_each):
+            neg_tr1, f1, neg_fr1 = factors[c]
             neg_er, pos_ei = sums[c]
             fr1, fi1 = f1[:, REAL, :], f1[:, IMAG, :]
             add_transposed(c, neg_er, looked_up_product(c, tr0, fr1))
+            after_each()
             add_transposed(c, pos_ei, looked_up_product(c, tr0, fi1))
+            after_each()
             add_transposed(c, neg_er, looked_up_product(c, ti0, fi1), last=last)
+            after_each()
             add_transposed(c, pos_ei, looked_up_product(c, ti0, neg_fr1[:]), last=last)
+            after_each()
 
         def finish(c):
             width = WIDTHS[c]
@@ -168,16 +187,16 @@ def tile_mseloss_kernel(tc, x, y, i_s, t_s, offs, out):
 
         prepare(0)
         real_gap_products(0)
-        target_products(0, last=False)
-        second_order(0)
         prepare(1)
-        imaginary_gap_products(0, last=True)
+        target_products(0, last=False, after_each=next_gap_block)
+        second_order(0)
+        imaginary_gap_products(0, last=True, after_each=next_gap_block)
         for c in range(1, len(WIDTHS)):
             real_gap_products(c)
-            imaginary_gap_products(c, last=False)
-            second_order(c)
-            finish(c - 1)
             if c + 1 < len(WIDTHS):
                 prepare(c + 1)
-            target_products(c, last=True)
+            imaginary_gap_products(c, last=False, after_each=nothing)
+            second_order(c)
+            finish(c - 1)
+            target_products(c, last=True, after_each=next_gap_block)
         finish(len(WIDTHS) - 1)

@@ -130,45 +130,51 @@ def tile_mseloss_kernel(tc, x, y, i_s, t_s, offs, out):
             if part == REAL:
                 nc.scalar.activation(neg_fr1[:, b], gap[:, 0:BLOCK], COPY, scale=-1.0)
 
-        def real_gap_products(c):
-            tr1, ti1 = t1[c][:, REAL, :], t1[c][:, IMAG, :]
+        opened = set()
+
+        def open_sums(c):
             neg_er = psum.tile([P, BANK], F32, name="neg_er")
             pos_ei = psum.tile([P, BANK], F32, name="pos_ei")
             sums[c] = (neg_er, pos_ei)
-            add_transposed(c, neg_er, looked_up_product(c, fr0, tr1), first=True)
-            add_transposed(c, pos_ei, looked_up_product(c, fr0, ti1), first=True)
+
+        def add_to_sum(c, part, term, last=False):
+            add_transposed(c, sums[c][part], term, first=(c, part) not in opened, last=last)
+            opened.add((c, part))
 
         def nothing():
             return None
 
+        def real_gap_products(c):
+            add_to_sum(c, REAL, looked_up_product(c, fr0, t1[c][:, REAL, :]))
+            add_to_sum(c, IMAG, looked_up_product(c, fr0, t1[c][:, IMAG, :]))
+
         def imaginary_gap_products(c, last, after_each):
             neg_tr1, f1, neg_fr1 = factors[c]
-            neg_er, pos_ei = sums[c]
-            add_transposed(c, pos_ei, looked_up_product(c, fi0, neg_tr1[:]), last=last)
+            add_to_sum(c, IMAG, looked_up_product(c, fi0, neg_tr1[:]), last=last)
             after_each()
-            add_transposed(c, neg_er, looked_up_product(c, fi0, t1[c][:, IMAG, :]), last=last)
+            add_to_sum(c, REAL, looked_up_product(c, fi0, t1[c][:, IMAG, :]), last=last)
             after_each()
 
         def second_order(c):
-            neg_er, pos_ei = sums[c]
             neg_is_r = negated(f"neg_is_r_{c}", i_s1[c][:, REAL, :], [P, WIDTHS[c]])
             neg_ts_i = negated(f"neg_ts_i_{c}", t_s1[c][:, IMAG, :], [P, WIDTHS[c]])
-            add_transposed(c, neg_er, t_s1[c][:, REAL, :])
-            add_transposed(c, neg_er, neg_is_r[:])
-            add_transposed(c, pos_ei, i_s1[c][:, IMAG, :])
-            add_transposed(c, pos_ei, neg_ts_i[:])
+            add_to_sum(c, REAL, t_s1[c][:, REAL, :])
+            add_to_sum(c, REAL, neg_is_r[:])
+            add_to_sum(c, IMAG, i_s1[c][:, IMAG, :])
+            add_to_sum(c, IMAG, neg_ts_i[:])
 
-        def target_products(c, last, after_each):
+        def real_target_products(c, after_each):
             neg_tr1, f1, neg_fr1 = factors[c]
-            neg_er, pos_ei = sums[c]
-            fr1, fi1 = f1[:, REAL, :], f1[:, IMAG, :]
-            add_transposed(c, neg_er, looked_up_product(c, tr0, fr1))
+            add_to_sum(c, REAL, looked_up_product(c, tr0, f1[:, REAL, :]))
             after_each()
-            add_transposed(c, pos_ei, looked_up_product(c, tr0, fi1))
+            add_to_sum(c, IMAG, looked_up_product(c, tr0, f1[:, IMAG, :]))
             after_each()
-            add_transposed(c, neg_er, looked_up_product(c, ti0, fi1), last=last)
+
+        def imaginary_target_products(c, last, after_each):
+            neg_tr1, f1, neg_fr1 = factors[c]
+            add_to_sum(c, REAL, looked_up_product(c, ti0, f1[:, IMAG, :]), last=last)
             after_each()
-            add_transposed(c, pos_ei, looked_up_product(c, ti0, neg_fr1[:]), last=last)
+            add_to_sum(c, IMAG, looked_up_product(c, ti0, neg_fr1[:]), last=last)
             after_each()
 
         def finish(c):
@@ -186,17 +192,28 @@ def tile_mseloss_kernel(tc, x, y, i_s, t_s, offs, out):
             nc.sync.dma_start(out[:, STARTS[c] : STARTS[c] + width], result[:])
 
         prepare(0)
+        open_sums(0)
         real_gap_products(0)
         prepare(1)
-        target_products(0, last=False, after_each=next_gap_block)
+        real_target_products(0, after_each=next_gap_block)
+        imaginary_target_products(0, last=False, after_each=next_gap_block)
         second_order(0)
         imaginary_gap_products(0, last=True, after_each=next_gap_block)
-        for c in range(1, len(WIDTHS)):
-            real_gap_products(c)
-            if c + 1 < len(WIDTHS):
-                prepare(c + 1)
-            imaginary_gap_products(c, last=False, after_each=nothing)
-            second_order(c)
-            finish(c - 1)
-            target_products(c, last=True, after_each=next_gap_block)
-        finish(len(WIDTHS) - 1)
+
+        open_sums(1)
+        real_gap_products(1)
+        prepare(2)
+        imaginary_gap_products(1, last=False, after_each=nothing)
+        second_order(1)
+        finish(0)
+        open_sums(2)
+        second_order(2)
+        real_target_products(1, after_each=next_gap_block)
+        imaginary_target_products(1, last=True, after_each=nothing)
+
+        real_gap_products(2)
+        imaginary_gap_products(2, last=False, after_each=nothing)
+        finish(1)
+        real_target_products(2, after_each=nothing)
+        imaginary_target_products(2, last=True, after_each=nothing)
+        finish(2)

@@ -12,6 +12,7 @@ assert sum(WIDTHS) == N
 F32 = mybir.dt.float32
 U16 = mybir.dt.uint16
 MULT = mybir.AluOpType.mult
+ADD = mybir.AluOpType.add
 SUB = mybir.AluOpType.subtract
 SQUARE = mybir.ActivationFunctionType.Square
 COPY = mybir.ActivationFunctionType.Copy
@@ -191,6 +192,40 @@ def tile_mseloss_kernel(tc, x, y, i_s, t_s, offs, out):
             nc.scalar.activation(result[:], total[:, 0:width], COPY)
             nc.sync.dma_start(out[:, STARTS[c] : STARTS[c] + width], result[:])
 
+        def back_to_rows(c, name, turned):
+            rows_first = psum.tile([P, BANK], F32, name=name)
+            add_transposed(c, rows_first, turned, first=True, last=True)
+            return rows_first[:, 0 : WIDTHS[c]]
+
+        def on_vector(c, name, in0, in1, op):
+            tile = held.tile([P, WIDTHS[c]], F32, name=name)
+            nc.vector.tensor_tensor(tile[:], in0, in1, op)
+            return tile
+
+        def last_piece(c):
+            width = WIDTHS[c]
+            neg_tr1, f1, neg_fr1 = factors[c]
+            tr1, ti1 = t1[c][:, REAL, :], t1[c][:, IMAG, :]
+            neg_er, part_of_ei = sums[c]
+            add_to_sum(c, IMAG, looked_up_product(c, fr0, ti1))
+            add_to_sum(c, IMAG, looked_up_product(c, fi0, neg_tr1[:]), last=True)
+            part_turned = held.tile([P, width], F32, name="part_turned")
+            nc.scalar.activation(part_turned[:], part_of_ei[:, 0:width], COPY)
+            part = back_to_rows(c, "gap", part_turned)
+            add_to_sum(c, REAL, looked_up_product(c, fr0, tr1))
+            add_to_sum(c, REAL, looked_up_product(c, fi0, ti1))
+            finish(c - 1)
+            add_to_sum(c, REAL, looked_up_product(c, tr0, f1[:, REAL, :]))
+            add_to_sum(c, REAL, looked_up_product(c, ti0, f1[:, IMAG, :]), last=True)
+            er_sq_turned = held.tile([P, width], F32, name="er_sq_turned")
+            nc.scalar.activation(er_sq_turned[:], neg_er[:, 0:width], SQUARE)
+            er_sq = back_to_rows(c, "total", er_sq_turned)
+            with_third = on_vector(c, "with_third", looked_up_product(c, tr0, f1[:, IMAG, :])[:], part, ADD)
+            pos_ei = on_vector(c, "pos_ei_rows", looked_up_product(c, ti0, neg_fr1[:])[:], with_third[:], ADD)
+            ei_sq = on_vector(c, "ei_sq_rows", pos_ei[:], pos_ei[:], MULT)
+            result = on_vector(c, "result_last", ei_sq[:], er_sq, ADD)
+            nc.sync.dma_start(out[:, STARTS[c] : STARTS[c] + width], result[:])
+
         prepare(0)
         open_sums(0)
         real_gap_products(0)
@@ -211,9 +246,4 @@ def tile_mseloss_kernel(tc, x, y, i_s, t_s, offs, out):
         real_target_products(1, after_each=next_gap_block)
         imaginary_target_products(1, last=True, after_each=nothing)
 
-        real_gap_products(2)
-        imaginary_gap_products(2, last=False, after_each=nothing)
-        finish(1)
-        real_target_products(2, after_each=nothing)
-        imaginary_target_products(2, last=True, after_each=nothing)
-        finish(2)
+        last_piece(2)

import concourse.mybir as mybir
from concourse.masks import make_identity

P = 128
S = 512
N = 1024
BLOCK = 128
BANK = 512
WIDTHS = (512, 384, 128)
STARTS = tuple(sum(WIDTHS[:c]) for c in range(len(WIDTHS)))
assert sum(WIDTHS) == N
F32 = mybir.dt.float32
U16 = mybir.dt.uint16
MULT = mybir.AluOpType.mult
ADD = mybir.AluOpType.add
SUB = mybir.AluOpType.subtract
SQUARE = mybir.ActivationFunctionType.Square
COPY = mybir.ActivationFunctionType.Copy
REAL, IMAG = 0, 1


def tile_mseloss_kernel(tc, x, y, i_s, t_s, offs, out):
    nc = tc.nc
    with (
        tc.tile_pool(name="held", bufs=1) as held,
        tc.tile_pool(name="ring", bufs=8) as ring,
        tc.psum_pool(name="psum", bufs=2) as psum,
    ):
        offsets = held.tile([P, N // 16], U16, name="offsets")

        def store_tile(name):
            return held.tile([P, S], F32, name=name)

        def pair_tiles(name):
            return [held.tile([P, 2, width], F32, name=f"{name}_{c}") for c, width in enumerate(WIDTHS)]

        def rows(source, first_block, c):
            columns = source[first_block * P : (first_block + 2) * P, STARTS[c] : STARTS[c] + WIDTHS[c]]
            return columns.rearrange("(b p) w -> p b w", p=P)

        est_r0, est_i0, tr0, ti0 = (store_tile(name) for name in ("est_r0", "est_i0", "tr0", "ti0"))
        est1, t1, i_s1, t_s1 = (pair_tiles(name) for name in ("est1", "t1", "i_s1", "t_s1"))

        nc.sync.dma_start(tr0[:], x[2 * P : 3 * P, :])
        nc.scalar.dma_start(est_r0[:], x[0:P, :])
        nc.sync.dma_start(offsets[:], offs)
        nc.scalar.dma_start(t1[0][:, REAL, :], y[2 * P : 3 * P, 0 : WIDTHS[0]])
        nc.sync.dma_start(t1[0][:, IMAG, :], y[3 * P : 4 * P, 0 : WIDTHS[0]])
        nc.scalar.dma_start(ti0[:], x[3 * P : 4 * P, :])
        nc.sync.dma_start(est_i0[:], x[P : 2 * P, :])
        nc.sync.dma_start(est1[0][:], rows(y, 0, 0))
        for c in range(len(WIDTHS)):
            if c + 1 < len(WIDTHS):
                nc.sync.dma_start(t1[c + 1][:], rows(y, 2, c + 1))
                nc.sync.dma_start(est1[c + 1][:], rows(y, 0, c + 1))
            nc.sync.dma_start(t_s1[c][:], rows(t_s, 0, c))
            nc.sync.dma_start(i_s1[c][:], rows(i_s, 0, c))

        identity = held.tile([P, P], F32, name="identity")
        minus = held.tile([P, P], F32, name="minus")
        make_identity(nc, identity[:])
        nc.gpsimd.tensor_scalar_mul(minus[:], identity[:], -1.0)

        fr0 = store_tile("fr0")
        fi0 = store_tile("fi0")
        nc.vector.tensor_tensor(fr0[:], est_r0[:], tr0[:], SUB)

        def blocks(c):
            return [slice(b * BLOCK, (b + 1) * BLOCK) for b in range(WIDTHS[c] // BLOCK)]

        def add_transposed(c, bank, term, first=False, last=False):
            for b in blocks(c):
                nc.tensor.matmul(
                    bank[:, b],
                    lhsT=term[:, b],
                    rhs=identity[:],
                    is_transpose=True,
                    start=first and b == blocks(c)[0],
                    stop=last and b == blocks(c)[-1],
                )

        def looked_up_product(c, window, factor):
            picks = offsets[:, STARTS[c] // 16 : (STARTS[c] + WIDTHS[c]) // 16]
            product = ring.tile([P, WIDTHS[c]], F32, name="product")
            nc.vector.tensor_tensor(product[:], window[:].indirect(picks), factor, MULT)
            return product

        def negated(name, source, shape):
            tile = held.tile(shape, F32, name=name)
            nc.scalar.activation(tile[:], source, COPY, scale=-1.0)
            return tile

        assert S == WIDTHS[0]
        neg_ti0 = negated("neg_ti0", ti0[:], [P, S])
        fi0_turned_sum = psum.tile([P, BANK], F32, name="gap")
        add_transposed(0, fi0_turned_sum, est_i0, first=True)
        add_transposed(0, fi0_turned_sum, neg_ti0, last=True)
        fi0_turned = store_tile("fi0_turned")
        nc.scalar.activation(fi0_turned[:], fi0_turned_sum[:], COPY)
        fi0_back = psum.tile([P, BANK], F32, name="gap")
        add_transposed(0, fi0_back, fi0_turned, first=True, last=True)
        nc.scalar.activation(fi0[:], fi0_back[:], COPY)

        factors = {}
        sums = {}

        def prepare(c):
            width = WIDTHS[c]
            neg_tr1 = negated(f"neg_tr1_{c}", t1[c][:, REAL, :], [P, width])
            f1 = held.tile([P, 2, width], F32, name=f"f1_{c}")
            if c == 0:
                nc.vector.tensor_tensor(f1[:], est1[c][:], t1[c][:], SUB)
                neg_fr1 = negated(f"neg_fr1_{c}", f1[:, REAL, :], [P, width])
            else:
                neg_fr1 = held.tile([P, width], F32, name=f"neg_fr1_{c}")
            factors[c] = (neg_tr1, f1, neg_fr1)

        gap_blocks = [(c, part, b) for c in range(1, len(WIDTHS)) for part in (REAL, IMAG) for b in blocks(c)]
        blocks_made = []

        def next_gap_block():
            if len(blocks_made) == len(gap_blocks):
                return
            c, part, b = gap_blocks[len(blocks_made)]
            blocks_made.append((c, part, b))
            neg_tr1, f1, neg_fr1 = factors[c]
            gap = psum.tile([P, BANK], F32, name="gap")
            nc.tensor.matmul(gap[:, 0:BLOCK], identity[:], est1[c][:, part, b], start=True, stop=False)
            nc.tensor.matmul(gap[:, 0:BLOCK], minus[:], t1[c][:, part, b], start=False, stop=True)
            nc.scalar.activation(f1[:, part, b], gap[:, 0:BLOCK], COPY)
            if part == REAL:
                nc.scalar.activation(neg_fr1[:, b], gap[:, 0:BLOCK], COPY, scale=-1.0)

        opened = set()

        def open_sums(c):
            neg_er = psum.tile([P, BANK], F32, name="neg_er")
            pos_ei = psum.tile([P, BANK], F32, name="pos_ei")
            sums[c] = (neg_er, pos_ei)

        def add_to_sum(c, part, term, last=False):
            add_transposed(c, sums[c][part], term, first=(c, part) not in opened, last=last)
            opened.add((c, part))

        def nothing():
            return None

        def real_gap_products(c):
            add_to_sum(c, REAL, looked_up_product(c, fr0, t1[c][:, REAL, :]))
            add_to_sum(c, IMAG, looked_up_product(c, fr0, t1[c][:, IMAG, :]))

        def imaginary_gap_products(c, last, after_each):
            neg_tr1, f1, neg_fr1 = factors[c]
            add_to_sum(c, IMAG, looked_up_product(c, fi0, neg_tr1[:]), last=last)
            after_each()
            add_to_sum(c, REAL, looked_up_product(c, fi0, t1[c][:, IMAG, :]), last=last)
            after_each()

        def second_order(c):
            neg_is_r = negated(f"neg_is_r_{c}", i_s1[c][:, REAL, :], [P, WIDTHS[c]])
            neg_ts_i = negated(f"neg_ts_i_{c}", t_s1[c][:, IMAG, :], [P, WIDTHS[c]])
            add_to_sum(c, REAL, t_s1[c][:, REAL, :])
            add_to_sum(c, REAL, neg_is_r[:])
            add_to_sum(c, IMAG, i_s1[c][:, IMAG, :])
            add_to_sum(c, IMAG, neg_ts_i[:])

        def real_target_products(c, after_each):
            neg_tr1, f1, neg_fr1 = factors[c]
            add_to_sum(c, REAL, looked_up_product(c, tr0, f1[:, REAL, :]))
            after_each()
            add_to_sum(c, IMAG, looked_up_product(c, tr0, f1[:, IMAG, :]))
            after_each()

        def imaginary_target_products(c, last, after_each):
            neg_tr1, f1, neg_fr1 = factors[c]
            add_to_sum(c, REAL, looked_up_product(c, ti0, f1[:, IMAG, :]), last=last)
            after_each()
            add_to_sum(c, IMAG, looked_up_product(c, ti0, neg_fr1[:]), last=last)
            after_each()

        def finish(c):
            width = WIDTHS[c]
            neg_er, pos_ei = sums[c]
            er_sq = held.tile([P, width], F32, name=f"er_sq_{c}")
            ei_sq = held.tile([P, width], F32, name=f"ei_sq_{c}")
            nc.scalar.activation(er_sq[:], neg_er[:, 0:width], SQUARE)
            nc.scalar.activation(ei_sq[:], pos_ei[:, 0:width], SQUARE)
            total = psum.tile([P, BANK], F32, name="total")
            add_transposed(c, total, er_sq, first=True)
            add_transposed(c, total, ei_sq, last=True)
            result = held.tile([P, width], F32, name=f"result_{c}")
            nc.scalar.activation(result[:], total[:, 0:width], COPY)
            nc.sync.dma_start(out[:, STARTS[c] : STARTS[c] + width], result[:])

        def back_to_rows(c, name, turned):
            rows_first = psum.tile([P, BANK], F32, name=name)
            add_transposed(c, rows_first, turned, first=True, last=True)
            return rows_first[:, 0 : WIDTHS[c]]

        def on_vector(c, name, in0, in1, op):
            tile = held.tile([P, WIDTHS[c]], F32, name=name)
            nc.vector.tensor_tensor(tile[:], in0, in1, op)
            return tile

        def last_piece(c):
            width = WIDTHS[c]
            neg_tr1, f1, neg_fr1 = factors[c]
            tr1, ti1 = t1[c][:, REAL, :], t1[c][:, IMAG, :]
            neg_er, part_of_ei = sums[c]
            add_to_sum(c, IMAG, looked_up_product(c, fr0, ti1))
            add_to_sum(c, IMAG, looked_up_product(c, fi0, neg_tr1[:]), last=True)
            part_turned = held.tile([P, width], F32, name="part_turned")
            nc.scalar.activation(part_turned[:], part_of_ei[:, 0:width], COPY)
            part = back_to_rows(c, "gap", part_turned)
            add_to_sum(c, REAL, looked_up_product(c, fr0, tr1))
            add_to_sum(c, REAL, looked_up_product(c, fi0, ti1))
            finish(c - 1)
            add_to_sum(c, REAL, looked_up_product(c, tr0, f1[:, REAL, :]))
            add_to_sum(c, REAL, looked_up_product(c, ti0, f1[:, IMAG, :]), last=True)
            er_sq_turned = held.tile([P, width], F32, name="er_sq_turned")
            nc.scalar.activation(er_sq_turned[:], neg_er[:, 0:width], SQUARE)
            er_sq = back_to_rows(c, "total", er_sq_turned)
            with_third = on_vector(c, "with_third", looked_up_product(c, tr0, f1[:, IMAG, :])[:], part, ADD)
            pos_ei = on_vector(c, "pos_ei_rows", looked_up_product(c, ti0, neg_fr1[:])[:], with_third[:], ADD)
            ei_sq = on_vector(c, "ei_sq_rows", pos_ei[:], pos_ei[:], MULT)
            result = on_vector(c, "result_last", ei_sq[:], er_sq, ADD)
            nc.sync.dma_start(out[:, STARTS[c] : STARTS[c] + width], result[:])

        prepare(0)
        open_sums(0)
        real_gap_products(0)
        prepare(1)
        real_target_products(0, after_each=next_gap_block)
        imaginary_target_products(0, last=False, after_each=next_gap_block)
        second_order(0)
        imaginary_gap_products(0, last=True, after_each=next_gap_block)

        open_sums(1)
        real_gap_products(1)
        prepare(2)
        imaginary_gap_products(1, last=False, after_each=nothing)
        second_order(1)
        finish(0)
        open_sums(2)
        second_order(2)
        real_target_products(1, after_each=next_gap_block)
        imaginary_target_products(1, last=True, after_each=nothing)

        last_piece(2)
